import numpy as np
import ml_dtypes


def mxq(x, axis, fmt="e4m3"):
    dtype, down = {"e4m3": (ml_dtypes.float8_e4m3fn, 7), "e5m2": (ml_dtypes.float8_e5m2, 14)}[fmt]
    v = np.moveaxis(np.asarray(x, np.float32).astype(ml_dtypes.bfloat16).astype(np.float64), axis, -1)
    blocks = v.reshape(v.shape[:-1] + (-1, 32))
    amax = np.abs(blocks).max(-1, keepdims=True)
    byte = np.maximum(np.where(amax > 0, np.frexp(amax)[1] - 1 + 127, 0) - down, 1)
    scale = np.exp2(byte - 127.0)
    codes = (blocks / scale).astype(np.float32).astype(dtype).astype(np.float64)
    return np.moveaxis((codes * scale).reshape(v.shape), -1, axis)


WIDE = False


def mx_kscale(k):
    if not WIDE:
        return np.ones(k)
    levels = np.array([10, -10, 5, -5, 0])
    a = np.random.permutation(np.resize(levels, k // 512 * 4)).reshape(k // 512, 4)
    idx = np.arange(k)
    return np.exp2(a[idx // 512, idx % 128 // 32])


BF16 = ml_dtypes.bfloat16


def bf(x):
    return np.asarray(x, np.float32).astype(BF16)


def f64(x):
    return np.asarray(x).astype(np.float64)


B, C, H, W, P = 1, 1024, 64, 32, 512
HP, WP = H // 2, W // 2
M = HP * WP
EPS = 1e-5


def maxpool2x2(x):
    return x.reshape(B, C, HP, 2, WP, 2).max(axis=(3, 5))


def setup_inputs():
    s = mx_kscale(C)
    return {'x': bf(np.random.standard_normal((B, C, H, W)) * s[None, :, None, None]),
            'wk': bf(np.random.standard_normal((P, C)) / np.sqrt(C) / s[None, :]),
            'bk': bf(np.random.standard_normal(P) * 0.1),
            'wv': bf(np.random.standard_normal((P, C)) / np.sqrt(C) / s[None, :]),
            'bv': bf(np.random.standard_normal(P) * 0.1),
            'k_gamma': bf(np.random.uniform(0.5, 1.5, P)),
            'k_beta': bf(np.random.standard_normal(P) * 0.1),
            'k_mean': bf(np.random.standard_normal(P) * 0.1),
            'k_var': bf(np.random.uniform(0.5, 1.5, P))}


def reference(x, wk, bk, wv, bv, k_gamma, k_beta, k_mean, k_var):
    xp = mxq(maxpool2x2(f64(x)).reshape(B, C, M), 1, 'e4m3')
    k = (mxq(f64(wk), 1, 'e4m3') @ xp) + f64(bk)[None, :, None]
    sc = f64(k_gamma) / np.sqrt(f64(k_var) + EPS)
    k = (k - f64(k_mean)[None, :, None]) * sc[None, :, None] + f64(k_beta)[None, :, None]
    v = (mxq(f64(wv), 1, 'e4m3') @ xp) + f64(bv)[None, :, None]
    return k.reshape(B, P, HP, WP), v.reshape(B, P, HP, WP)

@@ -1,0 +1,193 @@
+from contextlib import ExitStack
+
+import concourse.mybir as mybir
+from concourse.masks import make_identity
+
+BF16 = mybir.dt.bfloat16
+F32 = mybir.dt.float32
+I32 = mybir.dt.int32
+U32 = mybir.dt.uint32
+U8 = mybir.dt.uint8
+FP8X4 = mybir.dt.float8_e4m3fn_x4
+ACT = mybir.ActivationFunctionType
+ALU = mybir.AluOpType
+
+P = 128
+HW = 2048
+M = 512
+EPS = 1e-5
+FLOPS = 2 * 1024 * 1024 * 512
+
+
+def tile_nonlocalnd_bn_pa_kernel(
+    tc, x, wk, bk, wv, bv, k_gamma, k_beta, k_mean, k_var, out_0, out_1
+):
+    nc = tc.nc
+    with ExitStack() as ctx:
+        keep = ctx.enter_context(tc.tile_pool(name="keep", bufs=1))
+        ps_tp = ctx.enter_context(tc.psum_pool(name="ps_tp", bufs=4))
+        ps_acc = ctx.enter_context(tc.psum_pool(name="ps_acc", bufs=3))
+        ps_prm = ctx.enter_context(tc.psum_pool(name="ps_prm", bufs=1))
+
+        rows = keep.tile([P, 512], BF16, name="rows")
+        nc.vector.memset(rows[:].bitcast(I32), 0)
+        for v, vec in enumerate((bk, bv, k_gamma, k_beta, k_mean, k_var)):
+            nc.scalar.dma_start(out=rows[v : v + 1, :], in_=vec.rearrange("(o n) -> o n", o=1))
+
+        ident = keep.tile([P, P], F32, name="ident")
+        make_identity(nc, ident[:])
+
+        xv = x.rearrange("b (s p e) h w -> p (b s) (e h w)", s=4, p=P, e=2)
+        x_sb = []
+        for s in range(4):
+            xs = keep.tile([P, 2 * HW], BF16, name="x%d" % s)
+            nc.sync.dma_start(out=xs[:], in_=xv[:, s, :])
+            x_sb.append(xs)
+
+        w_sb = []
+        for wi, w in enumerate((wk, wv)):
+            ws = keep.tile([P, 4, 1024], BF16, name="w%d" % wi)
+            wview = w.rearrange("(p r) c -> p r c", r=4)
+            for j in range(2):
+                nc.sync.dma_start(out=ws[:, 2 * j : 2 * j + 2, :], in_=wview[:, 2 * j : 2 * j + 2, :])
+            w_sb.append(ws)
+
+        x_codes = keep.tile([P, 2, M], U32, name="x_codes", align_bytes=64)
+        x_scales = keep.tile([P, 2, M], U8, name="x_scales", align_bytes=64)
+        w_codes = keep.tile([P, 8, 2, P], U32, name="w_codes", align_bytes=64)
+        w_scales = keep.tile([P, 8, 2, P], U8, name="w_scales", align_bytes=64)
+        y_sb = [keep.tile([P, 4, 1024], BF16, name="y%d" % g) for g in range(2)]
+        xg_sb = [keep.tile([P, M, 4], BF16, name="xg%d" % g, align_bytes=64) for g in range(2)]
+        wg_sb = [keep.tile([P, 2, 1024], BF16, name="wg%d" % j, align_bytes=64) for j in range(4)]
+        res_sb = [keep.tile([P, 2, M], F32, name="res%d" % j) for j in range(4)]
+
+        def pool_rows(s):
+            g, u = divmod(s, 2)
+            xa = x_sb[s][:].rearrange("p (a d w) -> p a d w", d=2, w=32)
+            nc.vector.tensor_max(
+                out=y_sb[g][:, 2 * u : 2 * u + 2, :].rearrange("p e (i w) -> p (e i) w", w=32),
+                in0=xa[:, :, 0, :],
+                in1=xa[:, :, 1, :],
+            )
+
+        def pool_cols(g):
+            yv = y_sb[g][:].rearrange("p t (m d) -> p m t d", d=2)
+            nc.vector.tensor_max(out=xg_sb[g][:], in0=yv[:, :, :, 0], in1=yv[:, :, :, 1])
+
+        def quant_x(g):
+            nc.vector.quantize_mx(
+                out=x_codes[:, g, :].bitcast(FP8X4),
+                scales=x_scales[:, g, :],
+                in_=xg_sb[g][:].rearrange("p m t -> p (m t)"),
+            )
+
+        def transpose_pair(j):
+            w32 = w_sb[j // 2][:].rearrange("p r c -> p (r c)").bitcast(F32)
+            for i in range(2):
+                r = 2 * (j % 2) + i
+                tp = ps_tp.tile([P, 2, 2, P], F32, name="tp")
+                for g in range(2):
+                    for u in range(2):
+                        c0 = 512 * r + 256 * g + 128 * u
+                        nc.tensor.transpose(tp[:, g, u, :], w32[:, c0 : c0 + P], ident[:])
+                nc.scalar.copy(
+                    out=wg_sb[j][:, i, :].bitcast(F32).rearrange("p (g o u) -> p g o u", g=2, u=2),
+                    in_=tp[:].rearrange("p g u o -> p g o u"),
+                )
+
+        def quant_w(j):
+            nc.vector.quantize_mx(
+                out=w_codes[:, 2 * j : 2 * j + 2, :, :].rearrange("p b g o -> p (b g o)").bitcast(FP8X4),
+                scales=w_scales[:, 2 * j : 2 * j + 2, :, :].rearrange("p b g o -> p (b g o)"),
+                in_=wg_sb[j][:].rearrange("p r c -> p (r c)"),
+            )
+
+        prm = keep.tile([P, 6, 4], F32, name="prm")
+        t_var = keep.tile([P, 4], F32, name="t_var")
+        t_std = keep.tile([P, 4], F32, name="t_std")
+        t_rstd = keep.tile([P, 4], F32, name="t_rstd")
+        k_sc = keep.tile([P, 4], F32, name="k_sc")
+        t_d = keep.tile([P, 4], F32, name="t_d")
+        t_ds = keep.tile([P, 4], F32, name="t_ds")
+        k_b = keep.tile([P, 4], F32, name="k_b")
+
+        def params():
+            zt = ps_prm.tile([P, 2, P], F32, name="zt")
+            r32 = rows[:].bitcast(F32).rearrange("p (q h) -> p h q", h=2)
+            for h in range(2):
+                nc.tensor.transpose(zt[:, h, :], r32[:, h, :], ident[:])
+            nc.vector.tensor_copy(
+                out=prm[:].rearrange("p v (h e) -> p v h e", e=2),
+                in_=zt[:].bitcast(BF16).rearrange("p h (v e) -> p v h e", e=2)[:, 0:6, :, :],
+            )
+            nc.vector.tensor_scalar_add(out=t_var[:], in0=prm[:, 5, :], scalar1=EPS)
+            nc.scalar.sqrt(out=t_std[:], in_=t_var[:])
+            nc.vector.tensor_sub(out=t_d[:], in0=prm[:, 0, :], in1=prm[:, 4, :])
+            nc.vector.reciprocal(out=t_rstd[:], in_=t_std[:])
+            nc.vector.tensor_mul(out=k_sc[:], in0=prm[:, 2, :], in1=t_rstd[:])
+            nc.vector.tensor_mul(out=t_ds[:], in0=t_d[:], in1=k_sc[:])
+            nc.vector.tensor_add(out=k_b[:], in0=t_ds[:], in1=prm[:, 3, :])
+
+        out_v = [o.rearrange("b (p r) h w -> (b p) r (h w)", r=4) for o in (out_0, out_1)]
+
+        def block(b):
+            wi, r = divmod(b, 4)
+            j, i = divmod(b, 2)
+            acc = ps_acc.tile([P, M], F32, name="acc")
+            for g in range(2):
+                nc.tensor.matmul_mx(
+                    out=acc[:],
+                    lhsT=w_codes[:, b, g, :].bitcast(FP8X4),
+                    lhsT_scale=w_scales[:, b, g, :],
+                    rhs=x_codes[:, g, :].bitcast(FP8X4),
+                    rhs_scale=x_scales[:, g, :],
+                    start=(g == 0),
+                    stop=(g == 1),
+                )
+            dst = res_sb[j][:, i, :]
+            if wi == 0:
+                if i == 0:
+                    nc.scalar.activation(out=dst, in_=acc[:], func=ACT.Identity,
+                                         bias=k_b[:, r : r + 1], scale=k_sc[:, r : r + 1])
+                else:
+                    nc.vector.tensor_scalar(out=dst, in0=acc[:], scalar1=k_sc[:, r : r + 1],
+                                            scalar2=k_b[:, r : r + 1], op0=ALU.mult, op1=ALU.add)
+            else:
+                if i == 0:
+                    nc.scalar.activation(out=dst, in_=acc[:], func=ACT.Identity, bias=prm[:, 1, r : r + 1])
+                else:
+                    nc.vector.tensor_scalar_add(out=dst, in0=acc[:], scalar1=prm[:, 1, r : r + 1])
+
+        def store(j):
+            r0 = 2 * (j % 2)
+            nc.sync.dma_start(out=out_v[j // 2][:, r0 : r0 + 2, :], in_=res_sb[j][:])
+
+        pool_rows(0)
+        params()
+        pool_rows(1)
+        pool_cols(0)
+        pool_rows(2)
+        quant_x(0)
+        pool_rows(3)
+        transpose_pair(0)
+        transpose_pair(1)
+        pool_cols(1)
+        quant_w(0)
+        quant_x(1)
+        transpose_pair(2)
+        transpose_pair(3)
+        quant_w(1)
+        block(0)
+        block(1)
+        store(0)
+        quant_w(2)
+        block(2)
+        block(3)
+        store(1)
+        quant_w(3)
+        block(4)
+        block(5)
+        store(2)
+        block(6)
+        block(7)
+        store(3)

@@ -24,6 +24,7 @@ def tile_nonlocalnd_bn_pa_kernel(
 ):
     nc = tc.nc
     with ExitStack() as ctx:
+        ctx.enter_context(tc.manual_schedule())
         keep = ctx.enter_context(tc.tile_pool(name="keep", bufs=1))
         ps_tp = ctx.enter_context(tc.psum_pool(name="ps_tp", bufs=4))
         ps_acc = ctx.enter_context(tc.psum_pool(name="ps_acc", bufs=3))
@@ -162,6 +163,9 @@ def tile_nonlocalnd_bn_pa_kernel(
             r0 = 2 * (j % 2)
             nc.sync.dma_start(out=out_v[j // 2][:, r0 : r0 + 2, :], in_=res_sb[j][:])
 
+        def store_block(b):
+            nc.sync.dma_start(out=out_v[b // 4][:, b % 4, :], in_=res_sb[b // 2][:, b % 2, :])
+
         pool_rows(0)
         params()
         pool_rows(1)
@@ -169,25 +173,24 @@ def tile_nonlocalnd_bn_pa_kernel(
         pool_rows(2)
         quant_x(0)
         pool_rows(3)
-        transpose_pair(0)
-        transpose_pair(1)
+        for j in range(4):
+            transpose_pair(j)
         pool_cols(1)
         quant_w(0)
         quant_x(1)
-        transpose_pair(2)
-        transpose_pair(3)
         quant_w(1)
+        quant_w(2)
         block(0)
         block(1)
         store(0)
-        quant_w(2)
+        quant_w(3)
         block(2)
         block(3)
         store(1)
-        quant_w(3)
         block(4)
         block(5)
         store(2)
         block(6)
+        store_block(6)
         block(7)
-        store(3)
+        store_block(7)

@@ -42,7 +42,11 @@ def tile_nonlocalnd_bn_pa_kernel(
         x_sb = []
         for s in range(4):
             xs = keep.tile([P, 2 * HW], BF16, name="x%d" % s)
-            nc.sync.dma_start(out=xs[:], in_=xv[:, s, :])
+            if s == 1:
+                for e in range(2):
+                    nc.sync.dma_start(out=xs[:, e * HW : (e + 1) * HW], in_=xv[:, s, e * HW : (e + 1) * HW])
+            else:
+                nc.sync.dma_start(out=xs[:], in_=xv[:, s, :])
             x_sb.append(xs)
 
         w_sb = []
@@ -67,6 +71,15 @@ def tile_nonlocalnd_bn_pa_kernel(
             xa = x_sb[s][:].rearrange("p (a d w) -> p a d w", d=2, w=32)
             nc.vector.tensor_max(
                 out=y_sb[g][:, 2 * u : 2 * u + 2, :].rearrange("p e (i w) -> p (e i) w", w=32),
+                in0=xa[:, :, 0, :],
+                in1=xa[:, :, 1, :],
+            )
+
+        def pool_rows_half(s, e):
+            g, u = divmod(s, 2)
+            xa = x_sb[s][:, e * HW : (e + 1) * HW].rearrange("p (a d w) -> p a d w", d=2, w=32)
+            nc.vector.tensor_max(
+                out=y_sb[g][:, 2 * u + e, :].rearrange("p (i w) -> p i w", w=32),
                 in0=xa[:, :, 0, :],
                 in1=xa[:, :, 1, :],
             )
@@ -112,7 +125,11 @@ def tile_nonlocalnd_bn_pa_kernel(
         t_ds = keep.tile([P, 4], F32, name="t_ds")
         k_b = keep.tile([P, 4], F32, name="k_b")
 
-        def params():
+        warm = keep.tile([P, 1], F32, name="warm")
+        nc.vector.memset(warm[:], 1.0)
+        nc.scalar.sqrt(out=warm[:], in_=warm[:])
+
+        def params_a():
             zt = ps_prm.tile([P, 2, P], F32, name="zt")
             r32 = rows[:].bitcast(F32).rearrange("p (q h) -> p h q", h=2)
             for h in range(2):
@@ -124,6 +141,8 @@ def tile_nonlocalnd_bn_pa_kernel(
             nc.vector.tensor_scalar_add(out=t_var[:], in0=prm[:, 5, :], scalar1=EPS)
             nc.scalar.sqrt(out=t_std[:], in_=t_var[:])
             nc.vector.tensor_sub(out=t_d[:], in0=prm[:, 0, :], in1=prm[:, 4, :])
+
+        def params_b():
             nc.vector.reciprocal(out=t_rstd[:], in_=t_std[:])
             nc.vector.tensor_mul(out=k_sc[:], in0=prm[:, 2, :], in1=t_rstd[:])
             nc.vector.tensor_mul(out=t_ds[:], in0=t_d[:], in1=k_sc[:])
@@ -159,17 +178,15 @@ def tile_nonlocalnd_bn_pa_kernel(
                 else:
                     nc.vector.tensor_scalar_add(out=dst, in0=acc[:], scalar1=prm[:, 1, r : r + 1])
 
-        def store(j):
-            r0 = 2 * (j % 2)
-            nc.sync.dma_start(out=out_v[j // 2][:, r0 : r0 + 2, :], in_=res_sb[j][:])
-
         def store_block(b):
             nc.sync.dma_start(out=out_v[b // 4][:, b % 4, :], in_=res_sb[b // 2][:, b % 2, :])
 
         pool_rows(0)
-        params()
-        pool_rows(1)
+        params_a()
+        pool_rows_half(1, 0)
+        pool_rows_half(1, 1)
         pool_cols(0)
+        params_b()
         pool_rows(2)
         quant_x(0)
         pool_rows(3)
@@ -181,16 +198,10 @@ def tile_nonlocalnd_bn_pa_kernel(
         quant_w(1)
         quant_w(2)
         block(0)
+        store_block(0)
         block(1)
-        store(0)
+        store_block(1)
         quant_w(3)
-        block(2)
-        block(3)
-        store(1)
-        block(4)
-        block(5)
-        store(2)
-        block(6)
-        store_block(6)
-        block(7)
-        store_block(7)
+        for b in range(2, 8):
+            block(b)
+            store_block(b)

@@ -130,7 +130,7 @@ def tile_nonlocalnd_bn_pa_kernel(
         nc.scalar.sqrt(out=warm[:], in_=warm[:])
 
         def params_a():
-            zt = ps_prm.tile([P, 2, P], F32, name="zt")
+            zt = ps_prm.tile([P, 2, P], F32, name="zt", tag="zt")
             r32 = rows[:].bitcast(F32).rearrange("p (q h) -> p h q", h=2)
             for h in range(2):
                 nc.tensor.transpose(zt[:, h, :], r32[:, h, :], ident[:])
@@ -150,20 +150,38 @@ def tile_nonlocalnd_bn_pa_kernel(
 
         out_v = [o.rearrange("b (p r) h w -> (b p) r (h w)", r=4) for o in (out_0, out_1)]
 
-        def block(b):
+        acc_of = {}
+
+        def one_pass(b, g):
+            if g == 0:
+                acc_of[b] = ps_acc.tile([P, M], F32, name="acc")
+            nc.tensor.matmul_mx(
+                out=acc_of[b][:],
+                lhsT=w_codes[:, b, g, :].bitcast(FP8X4),
+                lhsT_scale=w_scales[:, b, g, :],
+                rhs=x_codes[:, g, :].bitcast(FP8X4),
+                rhs_scale=x_scales[:, g, :],
+                start=(g == 0),
+                stop=(g == 1),
+            )
+
+        def warm_up(n):
+            scratch = ps_prm.tile([P, M], F32, name="scratch", tag="zt")
+            for k in range(n):
+                nc.tensor.matmul_mx(
+                    out=scratch[:],
+                    lhsT=x_codes[:, 0, 0:P].bitcast(FP8X4),
+                    lhsT_scale=x_scales[:, 0, 0:P],
+                    rhs=x_codes[:, 0, :].bitcast(FP8X4),
+                    rhs_scale=x_scales[:, 0, :],
+                    start=True,
+                    stop=True,
+                )
+
+        def leave(b):
             wi, r = divmod(b, 4)
             j, i = divmod(b, 2)
-            acc = ps_acc.tile([P, M], F32, name="acc")
-            for g in range(2):
-                nc.tensor.matmul_mx(
-                    out=acc[:],
-                    lhsT=w_codes[:, b, g, :].bitcast(FP8X4),
-                    lhsT_scale=w_scales[:, b, g, :],
-                    rhs=x_codes[:, g, :].bitcast(FP8X4),
-                    rhs_scale=x_scales[:, g, :],
-                    start=(g == 0),
-                    stop=(g == 1),
-                )
+            acc = acc_of[b]
             dst = res_sb[j][:, i, :]
             if wi == 0:
                 if i == 0:
@@ -190,18 +208,26 @@ def tile_nonlocalnd_bn_pa_kernel(
         pool_rows(2)
         quant_x(0)
         pool_rows(3)
-        for j in range(4):
+        for j in range(3):
             transpose_pair(j)
+        warm_up(3)
+        transpose_pair(3)
         pool_cols(1)
         quant_w(0)
         quant_x(1)
         quant_w(1)
         quant_w(2)
-        block(0)
+        one_pass(0, 0)
+        one_pass(1, 0)
+        one_pass(0, 1)
+        leave(0)
         store_block(0)
-        block(1)
+        one_pass(1, 1)
+        leave(1)
         store_block(1)
         quant_w(3)
         for b in range(2, 8):
-            block(b)
+            one_pass(b, 0)
+            one_pass(b, 1)
+            leave(b)
             store_block(b)

@@ -38,16 +38,16 @@ def tile_nonlocalnd_bn_pa_kernel(
         ident = keep.tile([P, P], F32, name="ident")
         make_identity(nc, ident[:])
 
-        xv = x.rearrange("b (s p e) h w -> p (b s) (e h w)", s=4, p=P, e=2)
-        x_sb = []
-        for s in range(4):
-            xs = keep.tile([P, 2 * HW], BF16, name="x%d" % s)
-            if s == 1:
-                for e in range(2):
-                    nc.sync.dma_start(out=xs[:, e * HW : (e + 1) * HW], in_=xv[:, s, e * HW : (e + 1) * HW])
-            else:
-                nc.sync.dma_start(out=xs[:], in_=xv[:, s, :])
-            x_sb.append(xs)
+        xv = x.rearrange("b (s p e) (a h) w -> p (b s) a e (h w)", s=4, p=P, e=2, a=2)
+        xw = x.rearrange("b (s p e) h w -> p (b s) (e h w)", s=4, p=P, e=2)
+        x_half = [keep.tile([P, 2, 2, HW // 2], BF16, name="xh%d" % s) for s in range(2)]
+        for a in range(2):
+            for s in range(2):
+                nc.sync.dma_start(out=x_half[s][:, a, :, :], in_=xv[:, s, a, :, :])
+        x_sb = {}
+        for s in (2, 3):
+            x_sb[s] = keep.tile([P, 2 * HW], BF16, name="x%d" % s)
+            nc.sync.dma_start(out=x_sb[s][:], in_=xw[:, s, :])
 
         w_sb = []
         for wi, w in enumerate((wk, wv)):
@@ -75,18 +75,17 @@ def tile_nonlocalnd_bn_pa_kernel(
                 in1=xa[:, :, 1, :],
             )
 
-        def pool_rows_half(s, e):
-            g, u = divmod(s, 2)
-            xa = x_sb[s][:, e * HW : (e + 1) * HW].rearrange("p (a d w) -> p a d w", d=2, w=32)
+        def pool_rows_half(s, a):
+            xa = x_half[s][:, a, :, :].rearrange("p e (i d w) -> p e i d w", d=2, w=32)
             nc.vector.tensor_max(
-                out=y_sb[g][:, 2 * u + e, :].rearrange("p (i w) -> p i w", w=32),
-                in0=xa[:, :, 0, :],
-                in1=xa[:, :, 1, :],
+                out=y_sb[0][:, 2 * s : 2 * s + 2, 512 * a : 512 * a + 512].rearrange("p e (i w) -> p e i w", w=32),
+                in0=xa[:, :, :, 0, :],
+                in1=xa[:, :, :, 1, :],
             )
 
-        def pool_cols(g):
-            yv = y_sb[g][:].rearrange("p t (m d) -> p m t d", d=2)
-            nc.vector.tensor_max(out=xg_sb[g][:], in0=yv[:, :, :, 0], in1=yv[:, :, :, 1])
+        def pool_cols(g, m0, m1):
+            yv = y_sb[g][:, :, 2 * m0 : 2 * m1].rearrange("p t (m d) -> p m t d", d=2)
+            nc.vector.tensor_max(out=xg_sb[g][:, m0:m1, :], in0=yv[:, :, :, 0], in1=yv[:, :, :, 1])
 
         def quant_x(g):
             nc.vector.quantize_mx(
@@ -199,20 +198,22 @@ def tile_nonlocalnd_bn_pa_kernel(
         def store_block(b):
             nc.sync.dma_start(out=out_v[b // 4][:, b % 4, :], in_=res_sb[b // 2][:, b % 2, :])
 
-        pool_rows(0)
-        params_a()
+        pool_rows_half(0, 0)
         pool_rows_half(1, 0)
+        pool_cols(0, 0, 256)
+        params_a()
+        pool_rows_half(0, 1)
         pool_rows_half(1, 1)
-        pool_cols(0)
+        pool_cols(0, 256, 512)
         params_b()
-        pool_rows(2)
         quant_x(0)
+        pool_rows(2)
         pool_rows(3)
-        for j in range(3):
+        warm_up(5)
+        for j in range(4):
             transpose_pair(j)
-        warm_up(3)
-        transpose_pair(3)
-        pool_cols(1)
+            warm_up(1)
+        pool_cols(1, 0, 512)
         quant_w(0)
         quant_x(1)
         quant_w(1)

@@ -38,16 +38,16 @@ def tile_nonlocalnd_bn_pa_kernel(
         ident = keep.tile([P, P], F32, name="ident")
         make_identity(nc, ident[:])
 
-        xv = x.rearrange("b (s p e) (a h) w -> p (b s) a e (h w)", s=4, p=P, e=2, a=2)
-        xw = x.rearrange("b (s p e) h w -> p (b s) (e h w)", s=4, p=P, e=2)
-        x_half = [keep.tile([P, 2, 2, HW // 2], BF16, name="xh%d" % s) for s in range(2)]
-        for a in range(2):
-            for s in range(2):
-                nc.sync.dma_start(out=x_half[s][:, a, :, :], in_=xv[:, s, a, :, :])
-        x_sb = {}
-        for s in (2, 3):
-            x_sb[s] = keep.tile([P, 2 * HW], BF16, name="x%d" % s)
-            nc.sync.dma_start(out=x_sb[s][:], in_=xw[:, s, :])
+        xv = x.rearrange("b (s p e) h w -> p (b s) (e h w)", s=4, p=P, e=2)
+        x_sb = []
+        for s in range(4):
+            xs = keep.tile([P, 2 * HW], BF16, name="x%d" % s)
+            if s == 1:
+                for e in range(2):
+                    nc.sync.dma_start(out=xs[:, e * HW : (e + 1) * HW], in_=xv[:, s, e * HW : (e + 1) * HW])
+            else:
+                nc.sync.dma_start(out=xs[:], in_=xv[:, s, :])
+            x_sb.append(xs)
 
         w_sb = []
         for wi, w in enumerate((wk, wv)):
@@ -75,17 +75,18 @@ def tile_nonlocalnd_bn_pa_kernel(
                 in1=xa[:, :, 1, :],
             )
 
-        def pool_rows_half(s, a):
-            xa = x_half[s][:, a, :, :].rearrange("p e (i d w) -> p e i d w", d=2, w=32)
+        def pool_rows_half(s, e):
+            g, u = divmod(s, 2)
+            xa = x_sb[s][:, e * HW : (e + 1) * HW].rearrange("p (a d w) -> p a d w", d=2, w=32)
             nc.vector.tensor_max(
-                out=y_sb[0][:, 2 * s : 2 * s + 2, 512 * a : 512 * a + 512].rearrange("p e (i w) -> p e i w", w=32),
-                in0=xa[:, :, :, 0, :],
-                in1=xa[:, :, :, 1, :],
+                out=y_sb[g][:, 2 * u + e, :].rearrange("p (i w) -> p i w", w=32),
+                in0=xa[:, :, 0, :],
+                in1=xa[:, :, 1, :],
             )
 
-        def pool_cols(g, m0, m1):
-            yv = y_sb[g][:, :, 2 * m0 : 2 * m1].rearrange("p t (m d) -> p m t d", d=2)
-            nc.vector.tensor_max(out=xg_sb[g][:, m0:m1, :], in0=yv[:, :, :, 0], in1=yv[:, :, :, 1])
+        def pool_cols(g):
+            yv = y_sb[g][:].rearrange("p t (m d) -> p m t d", d=2)
+            nc.vector.tensor_max(out=xg_sb[g][:], in0=yv[:, :, :, 0], in1=yv[:, :, :, 1])
 
         def quant_x(g):
             nc.vector.quantize_mx(
@@ -167,15 +168,8 @@ def tile_nonlocalnd_bn_pa_kernel(
         def warm_up(n):
             scratch = ps_prm.tile([P, M], F32, name="scratch", tag="zt")
             for k in range(n):
-                nc.tensor.matmul_mx(
-                    out=scratch[:],
-                    lhsT=x_codes[:, 0, 0:P].bitcast(FP8X4),
-                    lhsT_scale=x_scales[:, 0, 0:P],
-                    rhs=x_codes[:, 0, :].bitcast(FP8X4),
-                    rhs_scale=x_scales[:, 0, :],
-                    start=True,
-                    stop=True,
-                )
+                nc.tensor.matmul(out=scratch[:], lhsT=y_sb[1][:, 0, 0:P], rhs=y_sb[1][:, 0, 0:M],
+                                 start=True, stop=True)
 
         def leave(b):
             wi, r = divmod(b, 4)
@@ -198,22 +192,21 @@ def tile_nonlocalnd_bn_pa_kernel(
         def store_block(b):
             nc.sync.dma_start(out=out_v[b // 4][:, b % 4, :], in_=res_sb[b // 2][:, b % 2, :])
 
-        pool_rows_half(0, 0)
-        pool_rows_half(1, 0)
-        pool_cols(0, 0, 256)
+        pool_rows(0)
         params_a()
-        pool_rows_half(0, 1)
+        pool_rows_half(1, 0)
         pool_rows_half(1, 1)
-        pool_cols(0, 256, 512)
+        pool_cols(0)
         params_b()
-        quant_x(0)
         pool_rows(2)
+        quant_x(0)
         pool_rows(3)
-        warm_up(5)
-        for j in range(4):
+        warm_up(3)
+        for j in range(3):
             transpose_pair(j)
             warm_up(1)
-        pool_cols(1, 0, 512)
+        transpose_pair(3)
+        pool_cols(1)
         quant_w(0)
         quant_x(1)
         quant_w(1)

@@ -85,8 +85,12 @@ def tile_nonlocalnd_bn_pa_kernel(
             )
 
         def pool_cols(g):
-            yv = y_sb[g][:].rearrange("p t (m d) -> p m t d", d=2)
-            nc.vector.tensor_max(out=xg_sb[g][:], in0=yv[:, :, :, 0], in1=yv[:, :, :, 1])
+            yv = y_sb[g][:].rearrange("p t (c i d) -> p c t i d", i=4, d=2)
+            nc.vector.tensor_max(
+                out=xg_sb[g][:].rearrange("p (c i) t -> p c t i", i=4),
+                in0=yv[:, :, :, :, 0],
+                in1=yv[:, :, :, :, 1],
+            )
 
         def quant_x(g):
             nc.vector.quantize_mx(
@@ -168,8 +172,15 @@ def tile_nonlocalnd_bn_pa_kernel(
         def warm_up(n):
             scratch = ps_prm.tile([P, M], F32, name="scratch", tag="zt")
             for k in range(n):
-                nc.tensor.matmul(out=scratch[:], lhsT=y_sb[1][:, 0, 0:P], rhs=y_sb[1][:, 0, 0:M],
-                                 start=True, stop=True)
+                nc.tensor.matmul_mx(
+                    out=scratch[:],
+                    lhsT=x_codes[:, 0, 0:P].bitcast(FP8X4),
+                    lhsT_scale=x_scales[:, 0, 0:P],
+                    rhs=x_codes[:, 0, :].bitcast(FP8X4),
+                    rhs_scale=x_scales[:, 0, :],
+                    start=True,
+                    stop=True,
+                )
 
         def leave(b):
             wi, r = divmod(b, 4)
@@ -201,10 +212,9 @@ def tile_nonlocalnd_bn_pa_kernel(
         pool_rows(2)
         quant_x(0)
         pool_rows(3)
-        warm_up(3)
         for j in range(3):
             transpose_pair(j)
-            warm_up(1)
+        warm_up(3)
         transpose_pair(3)
         pool_cols(1)
         quant_w(0)

@@ -32,8 +32,11 @@ def tile_nonlocalnd_bn_pa_kernel(
 
         rows = keep.tile([P, 512], BF16, name="rows")
         nc.vector.memset(rows[:].bitcast(I32), 0)
-        for v, vec in enumerate((bk, bv, k_gamma, k_beta, k_mean, k_var)):
+        def load_vector(v, vec):
             nc.scalar.dma_start(out=rows[v : v + 1, :], in_=vec.rearrange("(o n) -> o n", o=1))
+
+        for v, vec in ((0, bk), (2, k_gamma), (3, k_beta), (4, k_mean), (5, k_var)):
+            load_vector(v, vec)
 
         ident = keep.tile([P, P], F32, name="ident")
         make_identity(nc, ident[:])
@@ -48,6 +51,8 @@ def tile_nonlocalnd_bn_pa_kernel(
             else:
                 nc.sync.dma_start(out=xs[:], in_=xv[:, s, :])
             x_sb.append(xs)
+            if s == 1:
+                load_vector(1, bv)
 
         w_sb = []
         for wi, w in enumerate((wk, wv)):
@@ -84,13 +89,25 @@ def tile_nonlocalnd_bn_pa_kernel(
                 in1=xa[:, :, 1, :],
             )
 
-        def pool_cols(g):
-            yv = y_sb[g][:].rearrange("p t (c i d) -> p c t i d", i=4, d=2)
+        def pool_cols(g, m0, m1):
+            yv = y_sb[g][:, :, 2 * m0 : 2 * m1].rearrange("p t (c i d) -> p c t i d", i=4, d=2)
             nc.vector.tensor_max(
-                out=xg_sb[g][:].rearrange("p (c i) t -> p c t i", i=4),
+                out=xg_sb[g][:, m0:m1, :].rearrange("p (c i) t -> p c t i", i=4),
                 in0=yv[:, :, :, :, 0],
                 in1=yv[:, :, :, :, 1],
             )
+
+        yr = keep.tile([P, M, 4], BF16, name="yr")
+
+        def regroup():
+            nc.scalar.copy(
+                out=yr[:].rearrange("p (c i) t -> p c t i", i=4),
+                in_=y_sb[0][:, :, M : 2 * M].rearrange("p t (c i) -> p c t i", i=4),
+            )
+
+        def pool_cols_regrouped():
+            yrv = yr[:].rearrange("p (m d) t -> p m d t", d=2)
+            nc.vector.tensor_max(out=xg_sb[0][:, M // 2 : M, :], in0=yrv[:, :, 0, :], in1=yrv[:, :, 1, :])
 
         def quant_x(g):
             nc.vector.quantize_mx(
@@ -126,7 +143,6 @@ def tile_nonlocalnd_bn_pa_kernel(
         t_rstd = keep.tile([P, 4], F32, name="t_rstd")
         k_sc = keep.tile([P, 4], F32, name="k_sc")
         t_d = keep.tile([P, 4], F32, name="t_d")
-        t_ds = keep.tile([P, 4], F32, name="t_ds")
         k_b = keep.tile([P, 4], F32, name="k_b")
 
         warm = keep.tile([P, 1], F32, name="warm")
@@ -138,19 +154,25 @@ def tile_nonlocalnd_bn_pa_kernel(
             r32 = rows[:].bitcast(F32).rearrange("p (q h) -> p h q", h=2)
             for h in range(2):
                 nc.tensor.transpose(zt[:, h, :], r32[:, h, :], ident[:])
-            nc.vector.tensor_copy(
+            nc.scalar.copy(
                 out=prm[:].rearrange("p v (h e) -> p v h e", e=2),
                 in_=zt[:].bitcast(BF16).rearrange("p h (v e) -> p v h e", e=2)[:, 0:6, :, :],
             )
-            nc.vector.tensor_scalar_add(out=t_var[:], in0=prm[:, 5, :], scalar1=EPS)
+            nc.scalar.add(out=t_var[:], in_=prm[:, 5, :], add=EPS)
             nc.scalar.sqrt(out=t_std[:], in_=t_var[:])
-            nc.vector.tensor_sub(out=t_d[:], in0=prm[:, 0, :], in1=prm[:, 4, :])
+            for r in range(4):
+                nc.scalar.activation(out=t_d[:, r : r + 1], in_=prm[:, 4, r : r + 1], func=ACT.Identity,
+                                     bias=prm[:, 0, r : r + 1], scale=-1.0)
 
         def params_b():
             nc.vector.reciprocal(out=t_rstd[:], in_=t_std[:])
-            nc.vector.tensor_mul(out=k_sc[:], in0=prm[:, 2, :], in1=t_rstd[:])
-            nc.vector.tensor_mul(out=t_ds[:], in0=t_d[:], in1=k_sc[:])
-            nc.vector.tensor_add(out=k_b[:], in0=t_ds[:], in1=prm[:, 3, :])
+
+        def params_c():
+            for r in range(4):
+                nc.scalar.activation(out=k_sc[:, r : r + 1], in_=prm[:, 2, r : r + 1], func=ACT.Copy,
+                                     scale=t_rstd[:, r : r + 1])
+                nc.scalar.activation(out=k_b[:, r : r + 1], in_=t_d[:, r : r + 1], func=ACT.Identity,
+                                     bias=prm[:, 3, r : r + 1], scale=k_sc[:, r : r + 1])
 
         out_v = [o.rearrange("b (p r) h w -> (b p) r (h w)", r=4) for o in (out_0, out_1)]
 
@@ -172,15 +194,8 @@ def tile_nonlocalnd_bn_pa_kernel(
         def warm_up(n):
             scratch = ps_prm.tile([P, M], F32, name="scratch", tag="zt")
             for k in range(n):
-                nc.tensor.matmul_mx(
-                    out=scratch[:],
-                    lhsT=x_codes[:, 0, 0:P].bitcast(FP8X4),
-                    lhsT_scale=x_scales[:, 0, 0:P],
-                    rhs=x_codes[:, 0, :].bitcast(FP8X4),
-                    rhs_scale=x_scales[:, 0, :],
-                    start=True,
-                    stop=True,
-                )
+                nc.tensor.matmul(out=scratch[:], lhsT=y_sb[1][:, 0, 0:P], rhs=y_sb[1][:, 0, 0:M],
+                                 start=True, stop=True)
 
         def leave(b):
             wi, r = divmod(b, 4)
@@ -207,16 +222,22 @@ def tile_nonlocalnd_bn_pa_kernel(
         params_a()
         pool_rows_half(1, 0)
         pool_rows_half(1, 1)
-        pool_cols(0)
+        regroup()
+        pool_cols(0, 0, 256)
         params_b()
+        params_c()
         pool_rows(2)
-        quant_x(0)
+        pool_cols_regrouped()
         pool_rows(3)
-        for j in range(3):
-            transpose_pair(j)
+        quant_x(0)
         warm_up(3)
-        transpose_pair(3)
-        pool_cols(1)
+        transpose_pair(0)
+        warm_up(1)
+        transpose_pair(1)
+        warm_up(1)
+        transpose_pair(2)
+        warm_up(1)
+        pool_cols(1, 0, 512)
         quant_w(0)
         quant_x(1)
         quant_w(1)
@@ -229,9 +250,29 @@ def tile_nonlocalnd_bn_pa_kernel(
         one_pass(1, 1)
         leave(1)
         store_block(1)
+        transpose_pair(3)
         quant_w(3)
-        for b in range(2, 8):
-            one_pass(b, 0)
-            one_pass(b, 1)
-            leave(b)
-            store_block(b)
+        one_pass(2, 0)
+        one_pass(2, 1)
+        leave(2)
+        store_block(2)
+        one_pass(3, 0)
+        one_pass(3, 1)
+        leave(3)
+        store_block(3)
+        one_pass(4, 0)
+        one_pass(4, 1)
+        leave(4)
+        store_block(4)
+        one_pass(5, 0)
+        one_pass(5, 1)
+        leave(5)
+        store_block(5)
+        one_pass(6, 0)
+        one_pass(6, 1)
+        leave(6)
+        store_block(6)
+        one_pass(7, 0)
+        one_pass(7, 1)
+        leave(7)
+        store_block(7)

@@ -27,40 +27,45 @@ def tile_nonlocalnd_bn_pa_kernel(
         ctx.enter_context(tc.manual_schedule())
         keep = ctx.enter_context(tc.tile_pool(name="keep", bufs=1))
         ps_tp = ctx.enter_context(tc.psum_pool(name="ps_tp", bufs=4))
-        ps_acc = ctx.enter_context(tc.psum_pool(name="ps_acc", bufs=3))
-        ps_prm = ctx.enter_context(tc.psum_pool(name="ps_prm", bufs=1))
+        ps_acc = ctx.enter_context(tc.psum_pool(name="ps_acc", bufs=4))
 
+        warm = keep.tile([P, 1], F32, name="warm")
+        nc.vector.memset(warm[:], 1.0)
+        nc.scalar.sqrt(out=warm[:], in_=warm[:])
         rows = keep.tile([P, 512], BF16, name="rows")
         nc.vector.memset(rows[:].bitcast(I32), 0)
-        def load_vector(v, vec):
-            nc.scalar.dma_start(out=rows[v : v + 1, :], in_=vec.rearrange("(o n) -> o n", o=1))
-
-        for v, vec in ((0, bk), (2, k_gamma), (3, k_beta), (4, k_mean), (5, k_var)):
-            load_vector(v, vec)
 
         ident = keep.tile([P, P], F32, name="ident")
         make_identity(nc, ident[:])
 
-        xv = x.rearrange("b (s p e) h w -> p (b s) (e h w)", s=4, p=P, e=2)
-        x_sb = []
-        for s in range(4):
-            xs = keep.tile([P, 2 * HW], BF16, name="x%d" % s)
-            if s == 1:
-                for e in range(2):
-                    nc.sync.dma_start(out=xs[:, e * HW : (e + 1) * HW], in_=xv[:, s, e * HW : (e + 1) * HW])
-            else:
-                nc.sync.dma_start(out=xs[:], in_=xv[:, s, :])
-            x_sb.append(xs)
-            if s == 1:
-                load_vector(1, bv)
+        xv = x.rearrange("b (s p e) h w -> p (b s) e (h w)", s=4, p=P, e=2)
+        x_sb = [keep.tile([P, 2, HW], BF16, name="x%d" % s) for s in range(4)]
+        w_sb = [keep.tile([P, 4, 1024], BF16, name="w%d" % wi) for wi in range(2)]
 
-        w_sb = []
-        for wi, w in enumerate((wk, wv)):
-            ws = keep.tile([P, 4, 1024], BF16, name="w%d" % wi)
-            wview = w.rearrange("(p r) c -> p r c", r=4)
-            for j in range(2):
-                nc.sync.dma_start(out=ws[:, 2 * j : 2 * j + 2, :], in_=wview[:, 2 * j : 2 * j + 2, :])
-            w_sb.append(ws)
+        def load_x(s, e0, e1, h0, h1):
+            nc.sync.dma_start(out=x_sb[s][:, e0:e1, h0:h1], in_=xv[:, s, e0:e1, h0:h1])
+
+        def load_w(j):
+            wi, half = divmod(j, 2)
+            wview = (wk, wv)[wi].rearrange("(p r) c -> p r c", r=4)
+            nc.sync.dma_start(out=w_sb[wi][:, 2 * half : 2 * half + 2, :], in_=wview[:, 2 * half : 2 * half + 2, :])
+
+        vectors = (bk, bv, k_gamma, k_beta, k_mean, k_var)
+
+        def load_vectors(v0):
+            for v in (v0, v0 + 1):
+                nc.sync.dma_start(out=rows[v : v + 1, :], in_=vectors[v].rearrange("(o n) -> o n", o=1))
+
+        load_x(0, 0, 1, 0, HW)
+        load_vectors(0)
+        load_x(0, 1, 2, 0, HW)
+        load_vectors(2)
+        load_x(1, 0, 2, 0, HW)
+        load_vectors(4)
+        load_x(2, 0, 2, 0, HW)
+        load_x(3, 0, 2, 0, HW)
+        for j in range(4):
+            load_w(j)
 
         x_codes = keep.tile([P, 2, M], U32, name="x_codes", align_bytes=64)
         x_scales = keep.tile([P, 2, M], U8, name="x_scales", align_bytes=64)
@@ -71,23 +76,11 @@ def tile_nonlocalnd_bn_pa_kernel(
         wg_sb = [keep.tile([P, 2, 1024], BF16, name="wg%d" % j, align_bytes=64) for j in range(4)]
         res_sb = [keep.tile([P, 2, M], F32, name="res%d" % j) for j in range(4)]
 
-        def pool_rows(s):
+        def pool_rows(s, e0, e1, h0, h1):
             g, u = divmod(s, 2)
-            xa = x_sb[s][:].rearrange("p (a d w) -> p a d w", d=2, w=32)
-            nc.vector.tensor_max(
-                out=y_sb[g][:, 2 * u : 2 * u + 2, :].rearrange("p e (i w) -> p (e i) w", w=32),
-                in0=xa[:, :, 0, :],
-                in1=xa[:, :, 1, :],
-            )
-
-        def pool_rows_half(s, e):
-            g, u = divmod(s, 2)
-            xa = x_sb[s][:, e * HW : (e + 1) * HW].rearrange("p (a d w) -> p a d w", d=2, w=32)
-            nc.vector.tensor_max(
-                out=y_sb[g][:, 2 * u + e, :].rearrange("p (i w) -> p i w", w=32),
-                in0=xa[:, :, 0, :],
-                in1=xa[:, :, 1, :],
-            )
+            xa = x_sb[s][:, e0:e1, h0:h1].rearrange("p e (i d w) -> p e i d w", d=2, w=32)
+            ya = y_sb[g][:, 2 * u + e0 : 2 * u + e1, h0 // 2 : h1 // 2].rearrange("p e (i w) -> p e i w", w=32)
+            nc.vector.tensor_max(out=ya, in0=xa[:, :, :, 0, :], in1=xa[:, :, :, 1, :])
 
         def pool_cols(g, m0, m1):
             yv = y_sb[g][:, :, 2 * m0 : 2 * m1].rearrange("p t (c i d) -> p c t i d", i=4, d=2)
@@ -109,12 +102,14 @@ def tile_nonlocalnd_bn_pa_kernel(
             yrv = yr[:].rearrange("p (m d) t -> p m d t", d=2)
             nc.vector.tensor_max(out=xg_sb[0][:, M // 2 : M, :], in0=yrv[:, :, 0, :], in1=yrv[:, :, 1, :])
 
-        def quant_x(g):
+        def quant_x(g, m0, m1):
             nc.vector.quantize_mx(
-                out=x_codes[:, g, :].bitcast(FP8X4),
-                scales=x_scales[:, g, :],
-                in_=xg_sb[g][:].rearrange("p m t -> p (m t)"),
+                out=x_codes[:, g, m0:m1].bitcast(FP8X4),
+                scales=x_scales[:, g, m0:m1],
+                in_=xg_sb[g][:, m0:m1, :].rearrange("p m t -> p (m t)"),
             )
+
+        tp_of = {}
 
         def transpose_pair(j):
             w32 = w_sb[j // 2][:].rearrange("p r c -> p (r c)").bitcast(F32)
@@ -125,10 +120,17 @@ def tile_nonlocalnd_bn_pa_kernel(
                     for u in range(2):
                         c0 = 512 * r + 256 * g + 128 * u
                         nc.tensor.transpose(tp[:, g, u, :], w32[:, c0 : c0 + P], ident[:])
-                nc.scalar.copy(
-                    out=wg_sb[j][:, i, :].bitcast(F32).rearrange("p (g o u) -> p g o u", g=2, u=2),
-                    in_=tp[:].rearrange("p g u o -> p g o u"),
-                )
+                tp_of[j, i] = tp
+
+        def copy_block(j, i):
+            nc.scalar.copy(
+                out=wg_sb[j][:, i, :].bitcast(F32).rearrange("p (g o u) -> p g o u", g=2, u=2),
+                in_=tp_of[j, i][:].rearrange("p g u o -> p g o u"),
+            )
+
+        def copy_pair(j):
+            for i in range(2):
+                copy_block(j, i)
 
         def quant_w(j):
             nc.vector.quantize_mx(
@@ -145,12 +147,8 @@ def tile_nonlocalnd_bn_pa_kernel(
         t_d = keep.tile([P, 4], F32, name="t_d")
         k_b = keep.tile([P, 4], F32, name="k_b")
 
-        warm = keep.tile([P, 1], F32, name="warm")
-        nc.vector.memset(warm[:], 1.0)
-        nc.scalar.sqrt(out=warm[:], in_=warm[:])
-
         def params_a():
-            zt = ps_prm.tile([P, 2, P], F32, name="zt", tag="zt")
+            zt = ps_tp.tile([P, 2, P], F32, name="zt", tag="tp")
             r32 = rows[:].bitcast(F32).rearrange("p (q h) -> p h q", h=2)
             for h in range(2):
                 nc.tensor.transpose(zt[:, h, :], r32[:, h, :], ident[:])
@@ -192,7 +190,7 @@ def tile_nonlocalnd_bn_pa_kernel(
             )
 
         def warm_up(n):
-            scratch = ps_prm.tile([P, M], F32, name="scratch", tag="zt")
+            scratch = ps_tp.tile([P, M], F32, name="scratch", tag="tp")
             for k in range(n):
                 nc.tensor.matmul(out=scratch[:], lhsT=y_sb[1][:, 0, 0:P], rhs=y_sb[1][:, 0, 0:M],
                                  start=True, stop=True)
@@ -218,61 +216,50 @@ def tile_nonlocalnd_bn_pa_kernel(
         def store_block(b):
             nc.sync.dma_start(out=out_v[b // 4][:, b % 4, :], in_=res_sb[b // 2][:, b % 2, :])
 
-        pool_rows(0)
+        def passes(b):
+            one_pass(b, 0)
+            one_pass(b, 1)
+
+        pool_rows(0, 0, 1, 0, HW)
+        pool_rows(0, 1, 2, 0, HW)
+        pool_rows(1, 0, 2, 0, HW)
         params_a()
-        pool_rows_half(1, 0)
-        pool_rows_half(1, 1)
         regroup()
         pool_cols(0, 0, 256)
+        pool_rows(2, 0, 2, 0, HW)
         params_b()
         params_c()
-        pool_rows(2)
-        pool_cols_regrouped()
-        pool_rows(3)
-        quant_x(0)
         warm_up(3)
-        transpose_pair(0)
-        warm_up(1)
-        transpose_pair(1)
-        warm_up(1)
-        transpose_pair(2)
-        warm_up(1)
-        pool_cols(1, 0, 512)
+        pool_cols_regrouped()
+        pool_rows(3, 0, 2, 0, HW)
+        quant_x(0, 0, M)
+        pool_cols(1, 0, 256)
+        for j in range(3):
+            transpose_pair(j)
+            copy_pair(j)
+            warm_up(1)
+        transpose_pair(3)
+        copy_block(3, 0)
+        pool_cols(1, 256, 512)
         quant_w(0)
-        quant_x(1)
-        quant_w(1)
-        quant_w(2)
-        one_pass(0, 0)
-        one_pass(1, 0)
-        one_pass(0, 1)
+        quant_x(1, 0, M)
+        passes(0)
+        passes(1)
         leave(0)
         store_block(0)
-        one_pass(1, 1)
+        copy_block(3, 1)
+        quant_w(1)
+        quant_w(2)
         leave(1)
         store_block(1)
-        transpose_pair(3)
-        quant_w(3)
-        one_pass(2, 0)
-        one_pass(2, 1)
+        passes(2)
         leave(2)
         store_block(2)
-        one_pass(3, 0)
-        one_pass(3, 1)
+        passes(3)
         leave(3)
         store_block(3)
-        one_pass(4, 0)
-        one_pass(4, 1)
-        leave(4)
-        store_block(4)
-        one_pass(5, 0)
-        one_pass(5, 1)
-        leave(5)
-        store_block(5)
-        one_pass(6, 0)
-        one_pass(6, 1)
-        leave(6)
-        store_block(6)
-        one_pass(7, 0)
-        one_pass(7, 1)
-        leave(7)
-        store_block(7)
+        quant_w(3)
+        for b in range(4, 8):
+            passes(b)
+            leave(b)
+            store_block(b)

@@ -31,7 +31,7 @@ def tile_nonlocalnd_bn_pa_kernel(
 
         warm = keep.tile([P, 1], F32, name="warm")
         nc.vector.memset(warm[:], 1.0)
-        nc.scalar.sqrt(out=warm[:], in_=warm[:])
+        nc.scalar.activation(out=warm[:], in_=warm[:], func=ACT.Abs_reciprocal_sqrt)
         rows = keep.tile([P, 512], BF16, name="rows")
         nc.vector.memset(rows[:].bitcast(I32), 0)
 
@@ -60,10 +60,12 @@ def tile_nonlocalnd_bn_pa_kernel(
         load_vectors(0)
         load_x(0, 1, 2, 0, HW)
         load_vectors(2)
-        load_x(1, 0, 2, 0, HW)
+        load_x(1, 0, 1, 0, HW)
         load_vectors(4)
-        load_x(2, 0, 2, 0, HW)
-        load_x(3, 0, 2, 0, HW)
+        load_x(1, 1, 2, 0, HW)
+        for s in range(2, 4):
+            for e in range(2):
+                load_x(s, e, e + 1, 0, HW)
         for j in range(4):
             load_w(j)
 
@@ -140,14 +142,12 @@ def tile_nonlocalnd_bn_pa_kernel(
             )
 
         prm = keep.tile([P, 6, 4], F32, name="prm")
-        t_var = keep.tile([P, 4], F32, name="t_var")
-        t_std = keep.tile([P, 4], F32, name="t_std")
         t_rstd = keep.tile([P, 4], F32, name="t_rstd")
         k_sc = keep.tile([P, 4], F32, name="k_sc")
         t_d = keep.tile([P, 4], F32, name="t_d")
         k_b = keep.tile([P, 4], F32, name="k_b")
 
-        def params_a():
+        def params():
             zt = ps_tp.tile([P, 2, P], F32, name="zt", tag="tp")
             r32 = rows[:].bitcast(F32).rearrange("p (q h) -> p h q", h=2)
             for h in range(2):
@@ -156,16 +156,11 @@ def tile_nonlocalnd_bn_pa_kernel(
                 out=prm[:].rearrange("p v (h e) -> p v h e", e=2),
                 in_=zt[:].bitcast(BF16).rearrange("p h (v e) -> p v h e", e=2)[:, 0:6, :, :],
             )
-            nc.scalar.add(out=t_var[:], in_=prm[:, 5, :], add=EPS)
-            nc.scalar.sqrt(out=t_std[:], in_=t_var[:])
+            nc.scalar.activation(out=t_rstd[:], in_=prm[:, 5, :], func=ACT.Abs_reciprocal_sqrt, bias=EPS)
             for r in range(4):
                 nc.scalar.activation(out=t_d[:, r : r + 1], in_=prm[:, 4, r : r + 1], func=ACT.Identity,
                                      bias=prm[:, 0, r : r + 1], scale=-1.0)
 
-        def params_b():
-            nc.vector.reciprocal(out=t_rstd[:], in_=t_std[:])
-
-        def params_c():
             for r in range(4):
                 nc.scalar.activation(out=k_sc[:, r : r + 1], in_=prm[:, 2, r : r + 1], func=ACT.Copy,
                                      scale=t_rstd[:, r : r + 1])
@@ -192,23 +187,23 @@ def tile_nonlocalnd_bn_pa_kernel(
         def warm_up(n):
             scratch = ps_tp.tile([P, M], F32, name="scratch", tag="tp")
             for k in range(n):
-                nc.tensor.matmul(out=scratch[:], lhsT=y_sb[1][:, 0, 0:P], rhs=y_sb[1][:, 0, 0:M],
+                nc.tensor.matmul(out=scratch[:], lhsT=y_sb[1][:, 2, 0:P], rhs=y_sb[1][:, 2, 0:M],
                                  start=True, stop=True)
 
-        def leave(b):
+        def leave(b, on_scalar):
             wi, r = divmod(b, 4)
             j, i = divmod(b, 2)
             acc = acc_of[b]
             dst = res_sb[j][:, i, :]
             if wi == 0:
-                if i == 0:
+                if on_scalar:
                     nc.scalar.activation(out=dst, in_=acc[:], func=ACT.Identity,
                                          bias=k_b[:, r : r + 1], scale=k_sc[:, r : r + 1])
                 else:
                     nc.vector.tensor_scalar(out=dst, in0=acc[:], scalar1=k_sc[:, r : r + 1],
                                             scalar2=k_b[:, r : r + 1], op0=ALU.mult, op1=ALU.add)
             else:
-                if i == 0:
+                if on_scalar:
                     nc.scalar.activation(out=dst, in_=acc[:], func=ACT.Identity, bias=prm[:, 1, r : r + 1])
                 else:
                     nc.vector.tensor_scalar_add(out=dst, in0=acc[:], scalar1=prm[:, 1, r : r + 1])
@@ -220,46 +215,47 @@ def tile_nonlocalnd_bn_pa_kernel(
             one_pass(b, 0)
             one_pass(b, 1)
 
-        pool_rows(0, 0, 1, 0, HW)
-        pool_rows(0, 1, 2, 0, HW)
-        pool_rows(1, 0, 2, 0, HW)
-        params_a()
+        for s in range(2):
+            for e in range(2):
+                pool_rows(s, e, e + 1, 0, HW)
         regroup()
+        params()
         pool_cols(0, 0, 256)
-        pool_rows(2, 0, 2, 0, HW)
-        params_b()
-        params_c()
-        warm_up(3)
+        pool_rows(2, 0, 1, 0, HW)
+        pool_rows(2, 1, 2, 0, HW)
         pool_cols_regrouped()
-        pool_rows(3, 0, 2, 0, HW)
+        pool_rows(3, 0, 1, 0, HW)
+        warm_up(3)
         quant_x(0, 0, M)
-        pool_cols(1, 0, 256)
+        pool_rows(3, 1, 2, 0, HW)
         for j in range(3):
             transpose_pair(j)
             copy_pair(j)
             warm_up(1)
         transpose_pair(3)
-        copy_block(3, 0)
+        copy_pair(3)
+        pool_cols(1, 0, 256)
         pool_cols(1, 256, 512)
         quant_w(0)
         quant_x(1, 0, M)
-        passes(0)
-        passes(1)
-        leave(0)
-        store_block(0)
-        copy_block(3, 1)
+        one_pass(0, 0)
+        one_pass(1, 0)
+        one_pass(0, 1)
+        one_pass(1, 1)
         quant_w(1)
-        quant_w(2)
-        leave(1)
+        leave(0, False)
+        store_block(0)
+        leave(1, True)
         store_block(1)
         passes(2)
-        leave(2)
-        store_block(2)
         passes(3)
-        leave(3)
-        store_block(3)
+        quant_w(2)
         quant_w(3)
+        leave(2, True)
+        store_block(2)
+        leave(3, True)
+        store_block(3)
         for b in range(4, 8):
             passes(b)
-            leave(b)
+            leave(b, b % 2 == 1)
             store_block(b)

@@ -50,22 +50,16 @@ def tile_nonlocalnd_bn_pa_kernel(
             wview = (wk, wv)[wi].rearrange("(p r) c -> p r c", r=4)
             nc.sync.dma_start(out=w_sb[wi][:, 2 * half : 2 * half + 2, :], in_=wview[:, 2 * half : 2 * half + 2, :])
 
+        half = HW // 2
         vectors = (bk, bv, k_gamma, k_beta, k_mean, k_var)
-
-        def load_vectors(v0):
-            for v in (v0, v0 + 1):
+        for q in range(4):
+            s, e = divmod(q, 2)
+            load_x(s, e, e + 1, 0, HW)
+            for v in range(2 * q, 2 * q + 2) if q < 3 else ():
                 nc.sync.dma_start(out=rows[v : v + 1, :], in_=vectors[v].rearrange("(o n) -> o n", o=1))
-
-        load_x(0, 0, 1, 0, HW)
-        load_vectors(0)
-        load_x(0, 1, 2, 0, HW)
-        load_vectors(2)
-        load_x(1, 0, 1, 0, HW)
-        load_vectors(4)
-        load_x(1, 1, 2, 0, HW)
-        for s in range(2, 4):
-            for e in range(2):
-                load_x(s, e, e + 1, 0, HW)
+        for h in range(2):
+            for s in range(2, 4):
+                load_x(s, 0, 2, half * h, half * h + half)
         for j in range(4):
             load_w(j)
 
@@ -73,36 +67,36 @@ def tile_nonlocalnd_bn_pa_kernel(
         x_scales = keep.tile([P, 2, M], U8, name="x_scales", align_bytes=64)
         w_codes = keep.tile([P, 8, 2, P], U32, name="w_codes", align_bytes=64)
         w_scales = keep.tile([P, 8, 2, P], U8, name="w_scales", align_bytes=64)
-        y_sb = [keep.tile([P, 4, 1024], BF16, name="y%d" % g) for g in range(2)]
+        y_sb = {(g, h): keep.tile([P, 4, 512], BF16, name="y%d%d" % (g, h)) for g in range(2) for h in range(2)}
         xg_sb = [keep.tile([P, M, 4], BF16, name="xg%d" % g, align_bytes=64) for g in range(2)]
         wg_sb = [keep.tile([P, 2, 1024], BF16, name="wg%d" % j, align_bytes=64) for j in range(4)]
         res_sb = [keep.tile([P, 2, M], F32, name="res%d" % j) for j in range(4)]
 
-        def pool_rows(s, e0, e1, h0, h1):
+        def pool_rows(s, e0, e1, h):
             g, u = divmod(s, 2)
-            xa = x_sb[s][:, e0:e1, h0:h1].rearrange("p e (i d w) -> p e i d w", d=2, w=32)
-            ya = y_sb[g][:, 2 * u + e0 : 2 * u + e1, h0 // 2 : h1 // 2].rearrange("p e (i w) -> p e i w", w=32)
+            xa = x_sb[s][:, e0:e1, half * h : half * h + half].rearrange("p e (i d w) -> p e i d w", d=2, w=32)
+            ya = y_sb[g, h][:, 2 * u + e0 : 2 * u + e1, :].rearrange("p e (i w) -> p e i w", w=32)
             nc.vector.tensor_max(out=ya, in0=xa[:, :, :, 0, :], in1=xa[:, :, :, 1, :])
 
-        def pool_cols(g, m0, m1):
-            yv = y_sb[g][:, :, 2 * m0 : 2 * m1].rearrange("p t (c i d) -> p c t i d", i=4, d=2)
+        def pool_cols(g, h):
+            yv = y_sb[g, h][:].rearrange("p t (c i d) -> p c t i d", i=4, d=2)
             nc.vector.tensor_max(
-                out=xg_sb[g][:, m0:m1, :].rearrange("p (c i) t -> p c t i", i=4),
+                out=xg_sb[g][:, 256 * h : 256 * h + 256, :].rearrange("p (c i) t -> p c t i", i=4),
                 in0=yv[:, :, :, :, 0],
                 in1=yv[:, :, :, :, 1],
             )
 
-        yr = keep.tile([P, M, 4], BF16, name="yr")
+        yr = [keep.tile([P, M, 4], BF16, name="yr%d" % g) for g in range(2)]
 
-        def regroup():
+        def regroup(g, h):
             nc.scalar.copy(
-                out=yr[:].rearrange("p (c i) t -> p c t i", i=4),
-                in_=y_sb[0][:, :, M : 2 * M].rearrange("p t (c i) -> p c t i", i=4),
+                out=yr[g][:].rearrange("p (c i) t -> p c t i", i=4),
+                in_=y_sb[g, h][:].rearrange("p t (c i) -> p c t i", i=4),
             )
 
-        def pool_cols_regrouped():
-            yrv = yr[:].rearrange("p (m d) t -> p m d t", d=2)
-            nc.vector.tensor_max(out=xg_sb[0][:, M // 2 : M, :], in0=yrv[:, :, 0, :], in1=yrv[:, :, 1, :])
+        def pool_cols_regrouped(g, h):
+            yrv = yr[g][:].rearrange("p (m d) t -> p m d t", d=2)
+            nc.vector.tensor_max(out=xg_sb[g][:, 256 * h : 256 * h + 256, :], in0=yrv[:, :, 0, :], in1=yrv[:, :, 1, :])
 
         def quant_x(g, m0, m1):
             nc.vector.quantize_mx(
@@ -157,15 +151,10 @@ def tile_nonlocalnd_bn_pa_kernel(
                 in_=zt[:].bitcast(BF16).rearrange("p h (v e) -> p v h e", e=2)[:, 0:6, :, :],
             )
             nc.scalar.activation(out=t_rstd[:], in_=prm[:, 5, :], func=ACT.Abs_reciprocal_sqrt, bias=EPS)
-            for r in range(4):
-                nc.scalar.activation(out=t_d[:, r : r + 1], in_=prm[:, 4, r : r + 1], func=ACT.Identity,
-                                     bias=prm[:, 0, r : r + 1], scale=-1.0)
-
-            for r in range(4):
-                nc.scalar.activation(out=k_sc[:, r : r + 1], in_=prm[:, 2, r : r + 1], func=ACT.Copy,
-                                     scale=t_rstd[:, r : r + 1])
-                nc.scalar.activation(out=k_b[:, r : r + 1], in_=t_d[:, r : r + 1], func=ACT.Identity,
-                                     bias=prm[:, 3, r : r + 1], scale=k_sc[:, r : r + 1])
+            nc.gpsimd.tensor_sub(out=t_d[:], in0=prm[:, 0, :], in1=prm[:, 4, :])
+            nc.gpsimd.tensor_mul(out=k_sc[:], in0=prm[:, 2, :], in1=t_rstd[:])
+            nc.gpsimd.tensor_mul(out=t_d[:], in0=t_d[:], in1=k_sc[:])
+            nc.gpsimd.tensor_add(out=k_b[:], in0=t_d[:], in1=prm[:, 3, :])
 
         out_v = [o.rearrange("b (p r) h w -> (b p) r (h w)", r=4) for o in (out_0, out_1)]
 
@@ -187,7 +176,7 @@ def tile_nonlocalnd_bn_pa_kernel(
         def warm_up(n):
             scratch = ps_tp.tile([P, M], F32, name="scratch", tag="tp")
             for k in range(n):
-                nc.tensor.matmul(out=scratch[:], lhsT=y_sb[1][:, 2, 0:P], rhs=y_sb[1][:, 2, 0:M],
+                nc.tensor.matmul(out=scratch[:], lhsT=y_sb[1, 0][:, 2, 0:P], rhs=y_sb[1, 0][:, 2, :],
                                  start=True, stop=True)
 
         def leave(b, on_scalar):
@@ -215,33 +204,34 @@ def tile_nonlocalnd_bn_pa_kernel(
             one_pass(b, 0)
             one_pass(b, 1)
 
+        params()
         for s in range(2):
             for e in range(2):
-                pool_rows(s, e, e + 1, 0, HW)
-        regroup()
-        params()
-        pool_cols(0, 0, 256)
-        pool_rows(2, 0, 1, 0, HW)
-        pool_rows(2, 1, 2, 0, HW)
-        pool_cols_regrouped()
-        pool_rows(3, 0, 1, 0, HW)
-        warm_up(3)
+                pool_rows(s, e, e + 1, 1)
+                pool_rows(s, e, e + 1, 0)
+        regroup(0, 1)
+        pool_cols(0, 0)
+        for s in range(2, 4):
+            pool_rows(s, 0, 2, 0)
+        regroup(1, 0)
+        pool_cols_regrouped(0, 1)
         quant_x(0, 0, M)
-        pool_rows(3, 1, 2, 0, HW)
+        warm_up(3)
+        for s in range(2, 4):
+            pool_rows(s, 0, 2, 1)
         for j in range(3):
             transpose_pair(j)
             copy_pair(j)
             warm_up(1)
-        transpose_pair(3)
-        copy_pair(3)
-        pool_cols(1, 0, 256)
-        pool_cols(1, 256, 512)
+        pool_cols(1, 1)
+        pool_cols_regrouped(1, 0)
         quant_w(0)
         quant_x(1, 0, M)
         one_pass(0, 0)
-        one_pass(1, 0)
+        transpose_pair(3)
+        copy_pair(3)
         one_pass(0, 1)
-        one_pass(1, 1)
+        passes(1)
         quant_w(1)
         leave(0, False)
         store_block(0)

@@ -179,6 +179,19 @@ def tile_nonlocalnd_bn_pa_kernel(
                 nc.tensor.matmul(out=scratch[:], lhsT=y_sb[1, 0][:, 2, 0:P], rhs=y_sb[1, 0][:, 2, :],
                                  start=True, stop=True)
 
+        def idle_passes(n):
+            for k in range(n):
+                idle = ps_acc.tile([P, M], F32, name="idle", tag="acc")
+                nc.tensor.matmul_mx(
+                    out=idle[:],
+                    lhsT=x_codes[:, 0, 0:P].bitcast(FP8X4),
+                    lhsT_scale=x_scales[:, 0, 0:P],
+                    rhs=x_codes[:, 0, :].bitcast(FP8X4),
+                    rhs_scale=x_scales[:, 0, :],
+                    start=True,
+                    stop=True,
+                )
+
         def leave(b, on_scalar):
             wi, r = divmod(b, 4)
             j, i = divmod(b, 2)
@@ -216,13 +229,13 @@ def tile_nonlocalnd_bn_pa_kernel(
         regroup(1, 0)
         pool_cols_regrouped(0, 1)
         quant_x(0, 0, M)
-        warm_up(3)
+        warm_up(6)
         for s in range(2, 4):
             pool_rows(s, 0, 2, 1)
         for j in range(3):
             transpose_pair(j)
             copy_pair(j)
-            warm_up(1)
+            idle_passes(2)
         pool_cols(1, 1)
         pool_cols_regrouped(1, 0)
         quant_w(0)

@@ -176,7 +176,7 @@ def tile_nonlocalnd_bn_pa_kernel(
         def warm_up(n):
             scratch = ps_tp.tile([P, M], F32, name="scratch", tag="tp")
             for k in range(n):
-                nc.tensor.matmul(out=scratch[:], lhsT=y_sb[1, 0][:, 2, 0:P], rhs=y_sb[1, 0][:, 2, :],
+                nc.tensor.matmul(out=scratch[:], lhsT=y_sb[1, 0][:, 0, 0:P], rhs=y_sb[1, 0][:, 0, :],
                                  start=True, stop=True)
 
         def idle_passes(n):
@@ -224,41 +224,46 @@ def tile_nonlocalnd_bn_pa_kernel(
                 pool_rows(s, e, e + 1, 0)
         regroup(0, 1)
         pool_cols(0, 0)
-        for s in range(2, 4):
-            pool_rows(s, 0, 2, 0)
+        pool_rows(2, 0, 2, 0)
+        warm_up(6)
+        pool_rows(3, 0, 2, 0)
         regroup(1, 0)
         pool_cols_regrouped(0, 1)
-        quant_x(0, 0, M)
-        warm_up(6)
         for s in range(2, 4):
             pool_rows(s, 0, 2, 1)
+        quant_x(0, 0, M)
         for j in range(3):
             transpose_pair(j)
             copy_pair(j)
-            idle_passes(2)
+            idle_passes(1)
         pool_cols(1, 1)
         pool_cols_regrouped(1, 0)
         quant_w(0)
         quant_x(1, 0, M)
-        one_pass(0, 0)
-        transpose_pair(3)
-        copy_pair(3)
-        one_pass(0, 1)
+        passes(0)
         passes(1)
+        transpose_pair(3)
         quant_w(1)
         leave(0, False)
         store_block(0)
         leave(1, True)
         store_block(1)
+        copy_pair(3)
         passes(2)
         passes(3)
         quant_w(2)
-        quant_w(3)
-        leave(2, True)
+        leave(2, False)
         store_block(2)
         leave(3, True)
         store_block(3)
-        for b in range(4, 8):
+        passes(4)
+        passes(5)
+        quant_w(3)
+        leave(4, False)
+        store_block(4)
+        leave(5, True)
+        store_block(5)
+        for b in range(6, 8):
             passes(b)
             leave(b, b % 2 == 1)
             store_block(b)

@@ -220,8 +220,8 @@ def tile_nonlocalnd_bn_pa_kernel(
         params()
         for s in range(2):
             for e in range(2):
-                pool_rows(s, e, e + 1, 1)
                 pool_rows(s, e, e + 1, 0)
+                pool_rows(s, e, e + 1, 1)
         regroup(0, 1)
         pool_cols(0, 0)
         pool_rows(2, 0, 2, 0)
@@ -235,7 +235,8 @@ def tile_nonlocalnd_bn_pa_kernel(
         for j in range(3):
             transpose_pair(j)
             copy_pair(j)
-            idle_passes(1)
+            if j < 2:
+                idle_passes(2)
         pool_cols(1, 1)
         pool_cols_regrouped(1, 0)
         quant_w(0)

from contextlib import ExitStack

import concourse.mybir as mybir
from concourse.masks import make_identity

BF16 = mybir.dt.bfloat16
F32 = mybir.dt.float32
I32 = mybir.dt.int32
U32 = mybir.dt.uint32
U8 = mybir.dt.uint8
FP8X4 = mybir.dt.float8_e4m3fn_x4
ACT = mybir.ActivationFunctionType
ALU = mybir.AluOpType

P = 128
HW = 2048
M = 512
EPS = 1e-5
FLOPS = 2 * 1024 * 1024 * 512


def tile_nonlocalnd_bn_pa_kernel(
    tc, x, wk, bk, wv, bv, k_gamma, k_beta, k_mean, k_var, out_0, out_1
):
    nc = tc.nc
    with ExitStack() as ctx:
        ctx.enter_context(tc.manual_schedule())
        keep = ctx.enter_context(tc.tile_pool(name="keep", bufs=1))
        ps_tp = ctx.enter_context(tc.psum_pool(name="ps_tp", bufs=4))
        ps_acc = ctx.enter_context(tc.psum_pool(name="ps_acc", bufs=4))

        warm = keep.tile([P, 1], F32, name="warm")
        nc.vector.memset(warm[:], 1.0)
        nc.scalar.activation(out=warm[:], in_=warm[:], func=ACT.Abs_reciprocal_sqrt)
        rows = keep.tile([P, 512], BF16, name="rows")
        nc.vector.memset(rows[:].bitcast(I32), 0)

        ident = keep.tile([P, P], F32, name="ident")
        make_identity(nc, ident[:])

        xv = x.rearrange("b (s p e) h w -> p (b s) e (h w)", s=4, p=P, e=2)
        x_sb = [keep.tile([P, 2, HW], BF16, name="x%d" % s) for s in range(4)]
        w_sb = [keep.tile([P, 4, 1024], BF16, name="w%d" % wi) for wi in range(2)]

        def load_x(s, e0, e1, h0, h1):
            nc.sync.dma_start(out=x_sb[s][:, e0:e1, h0:h1], in_=xv[:, s, e0:e1, h0:h1])

        def load_w(j):
            wi, half = divmod(j, 2)
            wview = (wk, wv)[wi].rearrange("(p r) c -> p r c", r=4)
            nc.sync.dma_start(out=w_sb[wi][:, 2 * half : 2 * half + 2, :], in_=wview[:, 2 * half : 2 * half + 2, :])

        half = HW // 2
        vectors = (bk, bv, k_gamma, k_beta, k_mean, k_var)
        for q in range(4):
            s, e = divmod(q, 2)
            load_x(s, e, e + 1, 0, HW)
            for v in range(2 * q, 2 * q + 2) if q < 3 else ():
                nc.sync.dma_start(out=rows[v : v + 1, :], in_=vectors[v].rearrange("(o n) -> o n", o=1))
        for h in range(2):
            for s in range(2, 4):
                load_x(s, 0, 2, half * h, half * h + half)
        for j in range(4):
            load_w(j)

        x_codes = keep.tile([P, 2, M], U32, name="x_codes", align_bytes=64)
        x_scales = keep.tile([P, 2, M], U8, name="x_scales", align_bytes=64)
        w_codes = keep.tile([P, 8, 2, P], U32, name="w_codes", align_bytes=64)
        w_scales = keep.tile([P, 8, 2, P], U8, name="w_scales", align_bytes=64)
        y_sb = {(g, h): keep.tile([P, 4, 512], BF16, name="y%d%d" % (g, h)) for g in range(2) for h in range(2)}
        xg_sb = [keep.tile([P, M, 4], BF16, name="xg%d" % g, align_bytes=64) for g in range(2)]
        wg_sb = [keep.tile([P, 2, 1024], BF16, name="wg%d" % j, align_bytes=64) for j in range(4)]
        res_sb = [keep.tile([P, 2, M], F32, name="res%d" % j) for j in range(4)]

        def pool_rows(s, e0, e1, h):
            g, u = divmod(s, 2)
            xa = x_sb[s][:, e0:e1, half * h : half * h + half].rearrange("p e (i d w) -> p e i d w", d=2, w=32)
            ya = y_sb[g, h][:, 2 * u + e0 : 2 * u + e1, :].rearrange("p e (i w) -> p e i w", w=32)
            nc.vector.tensor_max(out=ya, in0=xa[:, :, :, 0, :], in1=xa[:, :, :, 1, :])

        def pool_cols(g, h):
            yv = y_sb[g, h][:].rearrange("p t (c i d) -> p c t i d", i=4, d=2)
            nc.vector.tensor_max(
                out=xg_sb[g][:, 256 * h : 256 * h + 256, :].rearrange("p (c i) t -> p c t i", i=4),
                in0=yv[:, :, :, :, 0],
                in1=yv[:, :, :, :, 1],
            )

        yr = [keep.tile([P, M, 4], BF16, name="yr%d" % g) for g in range(2)]

        def regroup(g, h):
            nc.scalar.copy(
                out=yr[g][:].rearrange("p (c i) t -> p c t i", i=4),
                in_=y_sb[g, h][:].rearrange("p t (c i) -> p c t i", i=4),
            )

        def pool_cols_regrouped(g, h):
            yrv = yr[g][:].rearrange("p (m d) t -> p m d t", d=2)
            nc.vector.tensor_max(out=xg_sb[g][:, 256 * h : 256 * h + 256, :], in0=yrv[:, :, 0, :], in1=yrv[:, :, 1, :])

        def quant_x(g, m0, m1):
            nc.vector.quantize_mx(
                out=x_codes[:, g, m0:m1].bitcast(FP8X4),
                scales=x_scales[:, g, m0:m1],
                in_=xg_sb[g][:, m0:m1, :].rearrange("p m t -> p (m t)"),
            )

        tp_of = {}

        def transpose_pair(j):
            w32 = w_sb[j // 2][:].rearrange("p r c -> p (r c)").bitcast(F32)
            for i in range(2):
                r = 2 * (j % 2) + i
                tp = ps_tp.tile([P, 2, 2, P], F32, name="tp")
                for g in range(2):
                    for u in range(2):
                        c0 = 512 * r + 256 * g + 128 * u
                        nc.tensor.transpose(tp[:, g, u, :], w32[:, c0 : c0 + P], ident[:])
                tp_of[j, i] = tp

        def copy_block(j, i):
            nc.scalar.copy(
                out=wg_sb[j][:, i, :].bitcast(F32).rearrange("p (g o u) -> p g o u", g=2, u=2),
                in_=tp_of[j, i][:].rearrange("p g u o -> p g o u"),
            )

        def copy_pair(j):
            for i in range(2):
                copy_block(j, i)

        def quant_w(j):
            nc.vector.quantize_mx(
                out=w_codes[:, 2 * j : 2 * j + 2, :, :].rearrange("p b g o -> p (b g o)").bitcast(FP8X4),
                scales=w_scales[:, 2 * j : 2 * j + 2, :, :].rearrange("p b g o -> p (b g o)"),
                in_=wg_sb[j][:].rearrange("p r c -> p (r c)"),
            )

        prm = keep.tile([P, 6, 4], F32, name="prm")
        t_rstd = keep.tile([P, 4], F32, name="t_rstd")
        k_sc = keep.tile([P, 4], F32, name="k_sc")
        t_d = keep.tile([P, 4], F32, name="t_d")
        k_b = keep.tile([P, 4], F32, name="k_b")

        def params():
            zt = ps_tp.tile([P, 2, P], F32, name="zt", tag="tp")
            r32 = rows[:].bitcast(F32).rearrange("p (q h) -> p h q", h=2)
            for h in range(2):
                nc.tensor.transpose(zt[:, h, :], r32[:, h, :], ident[:])
            nc.scalar.copy(
                out=prm[:].rearrange("p v (h e) -> p v h e", e=2),
                in_=zt[:].bitcast(BF16).rearrange("p h (v e) -> p v h e", e=2)[:, 0:6, :, :],
            )
            nc.scalar.activation(out=t_rstd[:], in_=prm[:, 5, :], func=ACT.Abs_reciprocal_sqrt, bias=EPS)
            nc.gpsimd.tensor_sub(out=t_d[:], in0=prm[:, 0, :], in1=prm[:, 4, :])
            nc.gpsimd.tensor_mul(out=k_sc[:], in0=prm[:, 2, :], in1=t_rstd[:])
            nc.gpsimd.tensor_mul(out=t_d[:], in0=t_d[:], in1=k_sc[:])
            nc.gpsimd.tensor_add(out=k_b[:], in0=t_d[:], in1=prm[:, 3, :])

        out_v = [o.rearrange("b (p r) h w -> (b p) r (h w)", r=4) for o in (out_0, out_1)]

        acc_of = {}

        def one_pass(b, g):
            if g == 0:
                acc_of[b] = ps_acc.tile([P, M], F32, name="acc")
            nc.tensor.matmul_mx(
                out=acc_of[b][:],
                lhsT=w_codes[:, b, g, :].bitcast(FP8X4),
                lhsT_scale=w_scales[:, b, g, :],
                rhs=x_codes[:, g, :].bitcast(FP8X4),
                rhs_scale=x_scales[:, g, :],
                start=(g == 0),
                stop=(g == 1),
            )

        def warm_up(n):
            scratch = ps_tp.tile([P, M], F32, name="scratch", tag="tp")
            for k in range(n):
                nc.tensor.matmul(out=scratch[:], lhsT=y_sb[1, 0][:, 0, 0:P], rhs=y_sb[1, 0][:, 0, :],
                                 start=True, stop=True)

        def idle_passes(n):
            for k in range(n):
                idle = ps_acc.tile([P, M], F32, name="idle", tag="acc")
                nc.tensor.matmul_mx(
                    out=idle[:],
                    lhsT=x_codes[:, 0, 0:P].bitcast(FP8X4),
                    lhsT_scale=x_scales[:, 0, 0:P],
                    rhs=x_codes[:, 0, :].bitcast(FP8X4),
                    rhs_scale=x_scales[:, 0, :],
                    start=True,
                    stop=True,
                )

        def leave(b, on_scalar):
            wi, r = divmod(b, 4)
            j, i = divmod(b, 2)
            acc = acc_of[b]
            dst = res_sb[j][:, i, :]
            if wi == 0:
                if on_scalar:
                    nc.scalar.activation(out=dst, in_=acc[:], func=ACT.Identity,
                                         bias=k_b[:, r : r + 1], scale=k_sc[:, r : r + 1])
                else:
                    nc.vector.tensor_scalar(out=dst, in0=acc[:], scalar1=k_sc[:, r : r + 1],
                                            scalar2=k_b[:, r : r + 1], op0=ALU.mult, op1=ALU.add)
            else:
                if on_scalar:
                    nc.scalar.activation(out=dst, in_=acc[:], func=ACT.Identity, bias=prm[:, 1, r : r + 1])
                else:
                    nc.vector.tensor_scalar_add(out=dst, in0=acc[:], scalar1=prm[:, 1, r : r + 1])

        def store_block(b):
            nc.sync.dma_start(out=out_v[b // 4][:, b % 4, :], in_=res_sb[b // 2][:, b % 2, :])

        def passes(b):
            one_pass(b, 0)
            one_pass(b, 1)

        params()
        for s in range(2):
            for e in range(2):
                pool_rows(s, e, e + 1, 0)
                pool_rows(s, e, e + 1, 1)
        regroup(0, 1)
        pool_cols(0, 0)
        pool_rows(2, 0, 2, 0)
        warm_up(6)
        pool_rows(3, 0, 2, 0)
        regroup(1, 0)
        pool_cols_regrouped(0, 1)
        for s in range(2, 4):
            pool_rows(s, 0, 2, 1)
        quant_x(0, 0, M)
        for j in range(3):
            transpose_pair(j)
            copy_pair(j)
            if j < 2:
                idle_passes(2)
        pool_cols(1, 1)
        pool_cols_regrouped(1, 0)
        quant_w(0)
        quant_x(1, 0, M)
        passes(0)
        passes(1)
        transpose_pair(3)
        quant_w(1)
        leave(0, False)
        store_block(0)
        leave(1, True)
        store_block(1)
        copy_pair(3)
        passes(2)
        passes(3)
        quant_w(2)
        leave(2, False)
        store_block(2)
        leave(3, True)
        store_block(3)
        passes(4)
        passes(5)
        quant_w(3)
        leave(4, False)
        store_block(4)
        leave(5, True)
        store_block(5)
        for b in range(6, 8):
            passes(b)
            leave(b, b % 2 == 1)
            store_block(b)
